import numpy as np
import ml_dtypes


def mxq(x, axis, fmt="e4m3"):
    dtype, down = {"e4m3": (ml_dtypes.float8_e4m3fn, 7), "e5m2": (ml_dtypes.float8_e5m2, 14)}[fmt]
    v = np.moveaxis(np.asarray(x, np.float32).astype(ml_dtypes.bfloat16).astype(np.float64), axis, -1)
    blocks = v.reshape(v.shape[:-1] + (-1, 32))
    amax = np.abs(blocks).max(-1, keepdims=True)
    byte = np.maximum(np.where(amax > 0, np.frexp(amax)[1] - 1 + 127, 0) - down, 1)
    scale = np.exp2(byte - 127.0)
    codes = (blocks / scale).astype(np.float32).astype(dtype).astype(np.float64)
    return np.moveaxis((codes * scale).reshape(v.shape), -1, axis)


WIDE = False


def mx_kscale(k):
    if not WIDE:
        return np.ones(k)
    levels = np.array([10, -10, 5, -5, 0])
    a = np.random.permutation(np.resize(levels, k // 512 * 4)).reshape(k // 512, 4)
    idx = np.arange(k)
    return np.exp2(a[idx // 512, idx % 128 // 32])


BF16 = ml_dtypes.bfloat16


def bf(x):
    return np.asarray(x, np.float32).astype(BF16)


def f64(x):
    return np.asarray(x).astype(np.float64)


E2M1 = np.array([0.0, 0.5, 1.0, 1.5, 2.0, 3.0, 4.0, 6.0, -0.0, -0.5, -1.0, -1.5, -2.0, -3.0, -4.0, -6.0])


def pack_weight(w, fmt):
    k, n = w.shape
    w = f64(bf(w)).reshape(k // 32, 32, n)
    amax = np.abs(w).max(1)
    if fmt == "e4m3":
        byte = np.frexp(amax)[1] - 1 + 127 - 7
    else:
        mant, ex = np.frexp(amax / 6.0)
        byte = np.where(mant > 0.5, ex, ex - 1) + 127
    byte = np.clip(np.where(amax > 0, byte, 1), 1, 254)
    scaled = (w * np.exp2(127.0 - byte)[:, None, :]).reshape(k, n).astype(np.float32)
    by_word = np.ascontiguousarray(scaled.reshape(k // 512, 128, 4, n).transpose(0, 1, 3, 2))
    if fmt == "e4m3":
        words = by_word.astype(ml_dtypes.float8_e4m3fn).view(np.uint8)
    else:
        c = by_word.astype(ml_dtypes.float4_e2m1fn).view(np.uint8) & 0xF
        words = c[..., 0::2] | (c[..., 1::2] << 4)
    return np.ascontiguousarray(words), np.ascontiguousarray(byte.astype(np.uint8).reshape(k // 512, 16, n))


def unpack_weight(words, scales, fmt):
    g, p, n, _ = words.shape
    if fmt == "e4m3":
        vals = np.ascontiguousarray(words).view(ml_dtypes.float8_e4m3fn).astype(np.float64)
    else:
        nib = np.empty((g, p, n, 4), np.uint8)
        nib[..., 0::2] = words & 0xF
        nib[..., 1::2] = words >> 4
        vals = E2M1[nib]
    vals = vals * np.repeat(np.exp2(scales.astype(np.float64) - 127.0), 8, axis=1)[..., None]
    return vals.transpose(0, 1, 3, 2).reshape(g * 512, n)

def pack4(w):
    words, scales = pack_weight(w, "e2m1")
    return words.reshape(words.shape[0], 128, -1), scales


def unpack4(words, scales):
    return unpack_weight(words.reshape(words.shape[0], 128, -1, 2), scales, "e2m1")


B, S, DIM, H, HD = 2, 64, 1024, 16, 128
E = H * HD


def rope_tables():
    inv_freq = 1.0 / (10000.0 ** (np.arange(0, HD, 2) / HD))
    freqs = np.outer(np.arange(S), inv_freq)
    emb = np.concatenate([freqs, freqs], axis=-1)
    return np.cos(emb)[None, None], np.sin(emb)[None, None]


def rotate_half(x):
    x1, x2 = np.split(x, 2, axis=-1)
    return np.concatenate([-x2, x1], axis=-1)


def setup_inputs():
    s = mx_kscale(DIM)
    cos, sin = rope_tables()
    query = bf(np.random.standard_normal((B, S, DIM)) * s)
    wq_words, wq_scales = pack4((np.random.standard_normal((E, DIM)) / np.sqrt(DIM) / s).T)
    return {"query": query,
            "wq_words": wq_words, "wq_scales": wq_scales,
            "bq": bf(np.random.standard_normal(E) * 0.1),
            "cos": bf(cos), "sin": bf(sin)}


def reference(query, wq_words, wq_scales, bq, cos, sin):
    q = (mxq(f64(query), 2, "e4m3") @ unpack4(wq_words, wq_scales)) + f64(bq)
    q = q.reshape(B, S, H, HD).transpose(0, 2, 1, 3)
    return q * f64(cos) + rotate_half(q) * f64(sin)

@@ -1,0 +1,158 @@
+import concourse.mybir as mybir
+from concourse.masks import make_identity
+
+F32 = mybir.dt.float32
+BF16 = mybir.dt.bfloat16
+I32 = mybir.dt.int32
+U32 = mybir.dt.uint32
+U8 = mybir.dt.uint8
+FP8X4 = mybir.dt.float8_e4m3fn_x4
+FP4X4 = mybir.dt.float4_e2m1fn_x4
+
+B, S, DIM, H, HD = 2, 64, 1024, 16, 128
+E = H * HD
+HALF = HD // 2
+P = 128
+PACK = 4
+K_PASS = P * PACK
+PASSES = DIM // K_PASS
+N_TILE = 512
+ROUNDS = E // N_TILE
+HEADS_PER_ROUND = N_TILE // HD
+BIAS_WORDS = N_TILE // P
+BIAS_BANKS = E // 2 // N_TILE
+
+FLOPS = 2 * B * S * DIM * E
+
+
+def tile_attention_pa_s_kernel(tc, query, wq_words, wq_scales, bq, cos, sin, out):
+    nc = tc.nc
+    with tc.tile_pool(name="keep", bufs=1) as keep, tc.tile_pool(name="rounds", bufs=ROUNDS) as rounds, tc.psum_pool(
+        name="flip", bufs=PASSES
+    ) as flip, tc.psum_pool(name="spreads", bufs=BIAS_BANKS) as spreads, tc.psum_pool(
+        name="sums", bufs=ROUNDS
+    ) as sums, tc.manual_schedule():
+
+        w_planes = keep.tile([P, PASSES, E], U8, align_bytes=64)
+        nc.vector.memset(w_planes[:].bitcast(I32), 0)
+
+        bias_cols = keep.tile([P, BIAS_BANKS, 2 * BIAS_WORDS], BF16)
+        nc.scalar.dma_start(out=bias_cols[:], in_=bq.rearrange("(c p i) -> p c i", c=BIAS_BANKS, p=P))
+
+        x_sb = keep.tile([P, DIM], BF16)
+        nc.scalar.dma_start(out=x_sb[:], in_=query.rearrange("b s k -> s b k"))
+
+        ident = keep.tile([P, P], F32)
+        make_identity(nc, ident[:])
+
+        scale_rows = wq_scales.rearrange("g (q r) n -> r q g n", r=PACK)
+        for r in range(PACK):
+            nc.sync.dma_start(out=w_planes[r:P:32, :, :].bitcast(I32), in_=scale_rows[r].bitcast(I32))
+
+        w_words = keep.tile([P, PASSES, 2 * E], U8, align_bytes=64)
+        words_by_partition = wq_words.rearrange("g p c -> p g c")
+        for half in range(2):
+            byte_cols = slice(half * E, (half + 1) * E)
+            nc.sync.dma_start(
+                out=w_words[:, :, byte_cols].bitcast(I32), in_=words_by_partition[:, :, byte_cols].bitcast(I32)
+            )
+
+        cos_sb = keep.tile([P, HD], BF16)
+        sin_sb = keep.tile([P, HD], BF16)
+        for table_sb, table in ((cos_sb, cos), (sin_sb, sin)):
+            rows = table.rearrange("a c s d -> (a c s) d")
+            nc.sync.dma_start(out=table_sb[:], in_=rows.unsqueeze(1).to_broadcast([S, B, HD]))
+
+        bias = keep.tile([P, E], BF16)
+        bias_words = bias_cols[:].bitcast(F32)
+
+        def spread_bias(c):
+            spread = spreads.tile([P, BIAS_WORDS, P], F32)
+            for w in range(BIAS_WORDS):
+                nc.tensor.transpose(spread[:, w, :], bias_words[:, c, w : w + 1].to_broadcast([P, P]), ident[:])
+            nc.scalar.copy(
+                out=bias[:, c * (E // BIAS_BANKS) : (c + 1) * (E // BIAS_BANKS)]
+                .bitcast(F32)
+                .rearrange("r (p w) -> r p w", w=BIAS_WORDS),
+                in_=spread[:].rearrange("r w p -> r p w"),
+            )
+
+        spread_bias(0)
+
+        x_words = x_sb[:].bitcast(F32)
+        grouped = keep.tile([P, PASSES, P * PACK], BF16, align_bytes=64)
+        x_codes = keep.tile([P, PASSES, P], U32, align_bytes=64)
+        x_planes = keep.tile([P, PASSES, P], U8, align_bytes=64)
+        for g in range(PASSES):
+            flipped = flip.tile([P, 2, P], F32)
+            for u in range(2):
+                nc.tensor.transpose(flipped[:, u, :], x_words[:, 256 * g + u : 256 * (g + 1) : 2], ident[:])
+            pairs_out = grouped[:, g, :].bitcast(F32).rearrange("p (r u) -> p r u", u=2)
+            pairs_in = flipped[:].rearrange("p u r -> p r u")
+            if g % 2 == 0:
+                nc.vector.tensor_copy(out=pairs_out, in_=pairs_in)
+            else:
+                nc.scalar.copy(out=pairs_out, in_=pairs_in)
+        for g in range(PASSES):
+            nc.vector.quantize_mx(out=x_codes[:, g, :].bitcast(FP8X4), scales=x_planes[:, g, :], in_=grouped[:, g, :])
+
+        spread_bias(1)
+
+        sin_other = keep.tile([P, 2, HALF], BF16)
+        for f in range(2):
+            nc.gpsimd.tensor_copy(out=sin_other[:, f, :], in_=sin_sb[:, (1 - f) * HALF : (2 - f) * HALF])
+        by_head = [P, HEADS_PER_ROUND, HD]
+        cos_by_head = cos_sb[:].unsqueeze(1).to_broadcast(by_head)
+        sin_by_head = sin_other[:].rearrange("p f j -> p (f j)").unsqueeze(1).to_broadcast(by_head)
+
+        def project(n):
+            acc = sums.tile([P, N_TILE], F32)
+            for g in range(PASSES):
+                nc.tensor.matmul_mx(
+                    out=acc[:],
+                    lhsT=x_codes[:, g, :].bitcast(FP8X4),
+                    lhsT_scale=x_planes[:, g, :],
+                    rhs=w_words[:, g, 2 * n * N_TILE : 2 * (n + 1) * N_TILE].bitcast(FP4X4),
+                    rhs_scale=w_planes[:, g, n * N_TILE : (n + 1) * N_TILE],
+                    start=(g == 0),
+                    stop=(g == PASSES - 1),
+                )
+            q_sb = rounds.tile([P, HEADS_PER_ROUND, HD], F32)
+            nc.vector.tensor_tensor(
+                out=q_sb[:].rearrange("p h d -> p (h d)"),
+                in0=acc[:],
+                in1=bias[:, n * N_TILE : (n + 1) * N_TILE],
+                op=mybir.AluOpType.add,
+            )
+            return q_sb
+
+        def multiply(q_sb):
+            by_sin = rounds.tile([P, HEADS_PER_ROUND, 2, HALF], F32)
+            nc.gpsimd.tensor_tensor(
+                out=by_sin[:].rearrange("p h f j -> p h (f j)"), in0=q_sb[:], in1=sin_by_head, op=mybir.AluOpType.mult
+            )
+            by_cos = rounds.tile([P, HEADS_PER_ROUND, 2, HALF], F32)
+            nc.vector.tensor_tensor(
+                out=by_cos[:].rearrange("p h f j -> p h (f j)"), in0=q_sb[:], in1=cos_by_head, op=mybir.AluOpType.mult
+            )
+            return by_cos, by_sin
+
+        def join_and_store(n, by_cos, by_sin):
+            for f, op in enumerate((mybir.AluOpType.subtract, mybir.AluOpType.add)):
+                nc.vector.tensor_tensor(
+                    out=by_cos[:, :, f, :], in0=by_cos[:, :, f, :], in1=by_sin[:, :, 1 - f, :], op=op
+                )
+            heads = slice(n * HEADS_PER_ROUND, (n + 1) * HEADS_PER_ROUND)
+            for b in range(B):
+                nc.sync.dma_start(
+                    out=out[b, heads].rearrange("h s d -> s h d"),
+                    in_=by_cos[b:P:B].rearrange("p h f j -> p h (f j)"),
+                )
+
+        products = []
+        for n in range(ROUNDS):
+            q_sb = project(n)
+            if n > 0:
+                join_and_store(n - 1, products[n - 1][0], products[n - 1][1])
+            products.append(multiply(q_sb))
+        join_and_store(ROUNDS - 1, products[ROUNDS - 1][0], products[ROUNDS - 1][1])

@@ -16,11 +16,9 @@ P = 128
 PACK = 4
 K_PASS = P * PACK
 PASSES = DIM // K_PASS
-N_TILE = 512
-ROUNDS = E // N_TILE
-HEADS_PER_ROUND = N_TILE // HD
-BIAS_WORDS = N_TILE // P
-BIAS_BANKS = E // 2 // N_TILE
+HEADS_PER_ROUND = 4
+ROUNDS = H // HEADS_PER_ROUND
+PSUM_BANKS = 8
 
 FLOPS = 2 * B * S * DIM * E
 
@@ -28,23 +26,33 @@ FLOPS = 2 * B * S * DIM * E
 def tile_attention_pa_s_kernel(tc, query, wq_words, wq_scales, bq, cos, sin, out):
     nc = tc.nc
     with tc.tile_pool(name="keep", bufs=1) as keep, tc.tile_pool(name="rounds", bufs=ROUNDS) as rounds, tc.psum_pool(
-        name="flip", bufs=PASSES
-    ) as flip, tc.psum_pool(name="spreads", bufs=BIAS_BANKS) as spreads, tc.psum_pool(
-        name="sums", bufs=ROUNDS
-    ) as sums, tc.manual_schedule():
-
-        w_planes = keep.tile([P, PASSES, E], U8, align_bytes=64)
-        nc.vector.memset(w_planes[:].bitcast(I32), 0)
-
-        bias_cols = keep.tile([P, BIAS_BANKS, 2 * BIAS_WORDS], BF16)
-        nc.scalar.dma_start(out=bias_cols[:], in_=bq.rearrange("(c p i) -> p c i", c=BIAS_BANKS, p=P))
+        name="banks", bufs=PSUM_BANKS
+    ) as banks, tc.manual_schedule():
 
         x_sb = keep.tile([P, DIM], BF16)
         nc.scalar.dma_start(out=x_sb[:], in_=query.rearrange("b s k -> s b k"))
 
+        bias_rows = keep.tile([P, HD], BF16)
+        nc.scalar.dma_start(
+            out=bias_rows[:], in_=bq.rearrange("(h d) -> h d", h=H).unsqueeze(0).to_broadcast([P // H, H, HD])
+        )
+
+        warm = keep.tile([P, 2], F32)
+        nc.gpsimd.memset(warm[:], 0.0)
         ident = keep.tile([P, P], F32)
         make_identity(nc, ident[:])
 
+        cos_sb = keep.tile([P, HD], BF16)
+        nc.gpsimd.dma_start(
+            out=cos_sb[:], in_=cos.rearrange("a c s d -> (a c s) d").unsqueeze(1).to_broadcast([S, B, HD])
+        )
+        sin_twice = keep.tile([P, 2 * HD], BF16)
+        nc.gpsimd.dma_start(
+            out=sin_twice[:], in_=sin.rearrange("a c s d -> (a c s) d").unsqueeze(1).to_broadcast([S, 2 * B, HD])
+        )
+
+        w_planes = keep.tile([P, PASSES, E], U8, align_bytes=64)
+        nc.vector.memset(w_planes[:].bitcast(I32), 0)
         scale_rows = wq_scales.rearrange("g (q r) n -> r q g n", r=PACK)
         for r in range(PACK):
             nc.sync.dma_start(out=w_planes[r:P:32, :, :].bitcast(I32), in_=scale_rows[r].bitcast(I32))
@@ -57,34 +65,23 @@ def tile_attention_pa_s_kernel(tc, query, wq_words, wq_scales, bq, cos, sin, out
                 out=w_words[:, :, byte_cols].bitcast(I32), in_=words_by_partition[:, :, byte_cols].bitcast(I32)
             )
 
-        cos_sb = keep.tile([P, HD], BF16)
-        sin_sb = keep.tile([P, HD], BF16)
-        for table_sb, table in ((cos_sb, cos), (sin_sb, sin)):
-            rows = table.rearrange("a c s d -> (a c s) d")
-            nc.sync.dma_start(out=table_sb[:], in_=rows.unsqueeze(1).to_broadcast([S, B, HD]))
+        sign = keep.tile([P, 1], F32)
+        nc.vector.memset(sign[0:HALF], 1.0)
+        nc.vector.memset(sign[HALF:P], -1.0)
+        ident_bf = keep.tile([P, P], BF16)
+        nc.vector.tensor_copy(out=ident_bf[:], in_=ident[:])
+        swap = keep.tile([P, 2, HALF], F32)
+        for f in range(2):
+            nc.vector.tensor_copy(out=swap[:, f, :], in_=ident[:, (1 - f) * HALF : (2 - f) * HALF])
 
-        bias = keep.tile([P, E], BF16)
-        bias_words = bias_cols[:].bitcast(F32)
-
-        def spread_bias(c):
-            spread = spreads.tile([P, BIAS_WORDS, P], F32)
-            for w in range(BIAS_WORDS):
-                nc.tensor.transpose(spread[:, w, :], bias_words[:, c, w : w + 1].to_broadcast([P, P]), ident[:])
-            nc.scalar.copy(
-                out=bias[:, c * (E // BIAS_BANKS) : (c + 1) * (E // BIAS_BANKS)]
-                .bitcast(F32)
-                .rearrange("r (p w) -> r p w", w=BIAS_WORDS),
-                in_=spread[:].rearrange("r w p -> r p w"),
-            )
-
-        spread_bias(0)
+        nc.scalar.activation(out=warm[:, 1:2], in_=warm[:, 0:1], func=mybir.ActivationFunctionType.Identity)
 
         x_words = x_sb[:].bitcast(F32)
         grouped = keep.tile([P, PASSES, P * PACK], BF16, align_bytes=64)
         x_codes = keep.tile([P, PASSES, P], U32, align_bytes=64)
         x_planes = keep.tile([P, PASSES, P], U8, align_bytes=64)
         for g in range(PASSES):
-            flipped = flip.tile([P, 2, P], F32)
+            flipped = banks.tile([P, 2, P], F32, tag="bank")
             for u in range(2):
                 nc.tensor.transpose(flipped[:, u, :], x_words[:, 256 * g + u : 256 * (g + 1) : 2], ident[:])
             pairs_out = grouped[:, g, :].bitcast(F32).rearrange("p (r u) -> p r u", u=2)
@@ -96,63 +93,93 @@ def tile_attention_pa_s_kernel(tc, query, wq_words, wq_scales, bq, cos, sin, out
         for g in range(PASSES):
             nc.vector.quantize_mx(out=x_codes[:, g, :].bitcast(FP8X4), scales=x_planes[:, g, :], in_=grouped[:, g, :])
 
-        spread_bias(1)
+        bias_flipped = banks.tile([P, P], BF16, tag="bank")
+        nc.tensor.transpose(bias_flipped[:], bias_rows[:], ident_bf[:])
+        bias_col = keep.tile([P, H], F32)
+        nc.scalar.copy(out=bias_col[:], in_=bias_flipped[:, 0:H])
 
-        sin_other = keep.tile([P, 2, HALF], BF16)
-        for f in range(2):
-            nc.gpsimd.tensor_copy(out=sin_other[:, f, :], in_=sin_sb[:, (1 - f) * HALF : (2 - f) * HALF])
-        by_head = [P, HEADS_PER_ROUND, HD]
-        cos_by_head = cos_sb[:].unsqueeze(1).to_broadcast(by_head)
-        sin_by_head = sin_other[:].rearrange("p f j -> p (f j)").unsqueeze(1).to_broadcast(by_head)
+        tables = keep.tile([P, 2, P], BF16)
+        by_head = [P, HEADS_PER_ROUND, P]
+        cos_by_head = tables[:, 0, :].unsqueeze(1).to_broadcast(by_head)
+        sin_by_head = tables[:, 1, :].unsqueeze(1).to_broadcast(by_head)
+
+        def flip_tables():
+            tables_flipped = banks.tile([P, 2, P], BF16, tag="bank")
+            nc.tensor.transpose(tables_flipped[:, 0, :], cos_sb[:], ident_bf[:])
+            nc.tensor.transpose(tables_flipped[:, 1, :], sin_twice[:, HALF : HALF + HD], ident_bf[:])
+            nc.vector.tensor_copy(out=tables[:, 0, :], in_=tables_flipped[:, 0, :])
+            nc.vector.tensor_scalar(
+                out=tables[:, 1, :],
+                in0=tables_flipped[:, 1, :],
+                scalar1=sign[:, 0:1],
+                scalar2=None,
+                op0=mybir.AluOpType.mult,
+            )
 
         def project(n):
-            acc = sums.tile([P, N_TILE], F32)
-            for g in range(PASSES):
-                nc.tensor.matmul_mx(
-                    out=acc[:],
-                    lhsT=x_codes[:, g, :].bitcast(FP8X4),
-                    lhsT_scale=x_planes[:, g, :],
-                    rhs=w_words[:, g, 2 * n * N_TILE : 2 * (n + 1) * N_TILE].bitcast(FP4X4),
-                    rhs_scale=w_planes[:, g, n * N_TILE : (n + 1) * N_TILE],
-                    start=(g == 0),
-                    stop=(g == PASSES - 1),
+            acc = banks.tile([P, HEADS_PER_ROUND, P], F32, tag="bank")
+            for j in range(HEADS_PER_ROUND):
+                h = n * HEADS_PER_ROUND + j
+                for g in range(PASSES):
+                    nc.tensor.matmul_mx(
+                        out=acc[:, j, :],
+                        lhsT=w_words[:, g, 2 * h * HD : 2 * (h + 1) * HD].bitcast(FP4X4),
+                        lhsT_scale=w_planes[:, g, h * HD : (h + 1) * HD],
+                        rhs=x_codes[:, g, :].bitcast(FP8X4),
+                        rhs_scale=x_planes[:, g, :],
+                        start=(g == 0),
+                        stop=(g == PASSES - 1),
+                    )
+            return acc
+
+        def add_bias(n, acc):
+            q_sb = rounds.tile([P, HEADS_PER_ROUND, P], F32)
+            for j in range(HEADS_PER_ROUND):
+                h = n * HEADS_PER_ROUND + j
+                nc.scalar.activation(
+                    out=q_sb[:, j, :],
+                    in_=acc[:, j, :],
+                    func=mybir.ActivationFunctionType.Identity,
+                    bias=bias_col[:, h : h + 1],
+                    scale=1.0,
                 )
-            q_sb = rounds.tile([P, HEADS_PER_ROUND, HD], F32)
-            nc.vector.tensor_tensor(
-                out=q_sb[:].rearrange("p h d -> p (h d)"),
-                in0=acc[:],
-                in1=bias[:, n * N_TILE : (n + 1) * N_TILE],
-                op=mybir.AluOpType.add,
-            )
             return q_sb
 
         def multiply(q_sb):
-            by_sin = rounds.tile([P, HEADS_PER_ROUND, 2, HALF], F32)
-            nc.gpsimd.tensor_tensor(
-                out=by_sin[:].rearrange("p h f j -> p h (f j)"), in0=q_sb[:], in1=sin_by_head, op=mybir.AluOpType.mult
-            )
-            by_cos = rounds.tile([P, HEADS_PER_ROUND, 2, HALF], F32)
-            nc.vector.tensor_tensor(
-                out=by_cos[:].rearrange("p h f j -> p h (f j)"), in0=q_sb[:], in1=cos_by_head, op=mybir.AluOpType.mult
-            )
+            by_cos = rounds.tile([P, HEADS_PER_ROUND, P], F32)
+            nc.vector.tensor_tensor(out=by_cos[:], in0=q_sb[:], in1=cos_by_head, op=mybir.AluOpType.mult)
+            by_sin = rounds.tile([P, HEADS_PER_ROUND, P], F32)
+            nc.vector.tensor_tensor(out=by_sin[:], in0=q_sb[:], in1=sin_by_head, op=mybir.AluOpType.mult)
             return by_cos, by_sin
 
-        def join_and_store(n, by_cos, by_sin):
-            for f, op in enumerate((mybir.AluOpType.subtract, mybir.AluOpType.add)):
-                nc.vector.tensor_tensor(
-                    out=by_cos[:, :, f, :], in0=by_cos[:, :, f, :], in1=by_sin[:, :, 1 - f, :], op=op
+        def join(by_cos, by_sin):
+            joined = banks.tile([P, HEADS_PER_ROUND, HD], F32, tag="bank")
+            for j in range(HEADS_PER_ROUND):
+                nc.tensor.matmul(
+                    out=joined[:, j, :], lhsT=by_cos[:, j, :], rhs=ident[:], is_transpose=True, start=True, stop=False
                 )
+                nc.tensor.matmul(
+                    out=joined[:, j, :],
+                    lhsT=by_sin[:, j, :],
+                    rhs=swap[:].rearrange("p f j -> p (f j)"),
+                    is_transpose=True,
+                    start=False,
+                    stop=True,
+                )
+            return joined
+
+        def store(n, joined):
+            out_sb = rounds.tile([P, HEADS_PER_ROUND, HD], F32)
+            nc.scalar.copy(out=out_sb[:], in_=joined[:])
             heads = slice(n * HEADS_PER_ROUND, (n + 1) * HEADS_PER_ROUND)
             for b in range(B):
-                nc.sync.dma_start(
-                    out=out[b, heads].rearrange("h s d -> s h d"),
-                    in_=by_cos[b:P:B].rearrange("p h f j -> p h (f j)"),
-                )
+                nc.sync.dma_start(out=out[b, heads].rearrange("h s d -> s h d"), in_=out_sb[b:P:B])
 
         products = []
         for n in range(ROUNDS):
-            q_sb = project(n)
-            if n > 0:
-                join_and_store(n - 1, products[n - 1][0], products[n - 1][1])
-            products.append(multiply(q_sb))
-        join_and_store(ROUNDS - 1, products[ROUNDS - 1][0], products[ROUNDS - 1][1])
+            acc = project(n)
+            if n == 0:
+                flip_tables()
+            products.append(multiply(add_bias(n, acc)))
+        for n in range(ROUNDS):
+            store(n, join(products[n][0], products[n][1]))

@@ -18,7 +18,7 @@ K_PASS = P * PACK
 PASSES = DIM // K_PASS
 HEADS_PER_ROUND = 4
 ROUNDS = H // HEADS_PER_ROUND
-PSUM_BANKS = 8
+PSUM_BANKS = 7
 
 FLOPS = 2 * B * S * DIM * E
 
@@ -27,7 +27,7 @@ def tile_attention_pa_s_kernel(tc, query, wq_words, wq_scales, bq, cos, sin, out
     nc = tc.nc
     with tc.tile_pool(name="keep", bufs=1) as keep, tc.tile_pool(name="rounds", bufs=ROUNDS) as rounds, tc.psum_pool(
         name="banks", bufs=PSUM_BANKS
-    ) as banks, tc.manual_schedule():
+    ) as banks, tc.psum_pool(name="idle", bufs=1) as idle, tc.manual_schedule():
 
         x_sb = keep.tile([P, DIM], BF16)
         nc.scalar.dma_start(out=x_sb[:], in_=query.rearrange("b s k -> s b k"))
@@ -37,33 +37,49 @@ def tile_attention_pa_s_kernel(tc, query, wq_words, wq_scales, bq, cos, sin, out
             out=bias_rows[:], in_=bq.rearrange("(h d) -> h d", h=H).unsqueeze(0).to_broadcast([P // H, H, HD])
         )
 
-        warm = keep.tile([P, 2], F32)
-        nc.gpsimd.memset(warm[:], 0.0)
-        ident = keep.tile([P, P], F32)
-        make_identity(nc, ident[:])
-
         cos_sb = keep.tile([P, HD], BF16)
-        nc.gpsimd.dma_start(
+        nc.scalar.dma_start(
             out=cos_sb[:], in_=cos.rearrange("a c s d -> (a c s) d").unsqueeze(1).to_broadcast([S, B, HD])
         )
         sin_twice = keep.tile([P, 2 * HD], BF16)
-        nc.gpsimd.dma_start(
+        nc.scalar.dma_start(
             out=sin_twice[:], in_=sin.rearrange("a c s d -> (a c s) d").unsqueeze(1).to_broadcast([S, 2 * B, HD])
         )
 
         w_planes = keep.tile([P, PASSES, E], U8, align_bytes=64)
         nc.vector.memset(w_planes[:].bitcast(I32), 0)
         scale_rows = wq_scales.rearrange("g (q r) n -> r q g n", r=PACK)
-        for r in range(PACK):
-            nc.sync.dma_start(out=w_planes[r:P:32, :, :].bitcast(I32), in_=scale_rows[r].bitcast(I32))
-
         w_words = keep.tile([P, PASSES, 2 * E], U8, align_bytes=64)
         words_by_partition = wq_words.rearrange("g p c -> p g c")
-        for half in range(2):
+
+        def load_scales(r):
+            nc.sync.dma_start(out=w_planes[r:P:32, :, :].bitcast(I32), in_=scale_rows[r].bitcast(I32))
+
+        def load_words(half):
             byte_cols = slice(half * E, (half + 1) * E)
             nc.sync.dma_start(
                 out=w_words[:, :, byte_cols].bitcast(I32), in_=words_by_partition[:, :, byte_cols].bitcast(I32)
             )
+
+        load_scales(0)
+        load_scales(1)
+        load_scales(2)
+        load_words(0)
+        load_scales(3)
+        load_words(1)
+
+        warm = keep.tile([P, 2], F32)
+        nc.gpsimd.memset(warm[:], 0.0)
+        ident = keep.tile([P, P], F32)
+        make_identity(nc, ident[:])
+
+        idle_bank = idle.tile([P, P], F32)
+
+        def keep_busy(times):
+            for i in range(times):
+                nc.tensor.matmul(out=idle_bank[:], lhsT=ident[:], rhs=ident[:], start=True, stop=True)
+
+        keep_busy(3)
 
         sign = keep.tile([P, 1], F32)
         nc.vector.memset(sign[0:HALF], 1.0)
@@ -93,11 +109,6 @@ def tile_attention_pa_s_kernel(tc, query, wq_words, wq_scales, bq, cos, sin, out
         for g in range(PASSES):
             nc.vector.quantize_mx(out=x_codes[:, g, :].bitcast(FP8X4), scales=x_planes[:, g, :], in_=grouped[:, g, :])
 
-        bias_flipped = banks.tile([P, P], BF16, tag="bank")
-        nc.tensor.transpose(bias_flipped[:], bias_rows[:], ident_bf[:])
-        bias_col = keep.tile([P, H], F32)
-        nc.scalar.copy(out=bias_col[:], in_=bias_flipped[:, 0:H])
-
         tables = keep.tile([P, 2, P], BF16)
         by_head = [P, HEADS_PER_ROUND, P]
         cos_by_head = tables[:, 0, :].unsqueeze(1).to_broadcast(by_head)
@@ -115,6 +126,15 @@ def tile_attention_pa_s_kernel(tc, query, wq_words, wq_scales, bq, cos, sin, out
                 scalar2=None,
                 op0=mybir.AluOpType.mult,
             )
+
+        flip_tables()
+
+        bias_flipped = banks.tile([P, P], BF16, tag="bank")
+        nc.tensor.transpose(bias_flipped[:], bias_rows[:], ident_bf[:])
+        bias_col = keep.tile([P, H], F32)
+        nc.scalar.copy(out=bias_col[:], in_=bias_flipped[:, 0:H])
+
+        keep_busy(3)
 
         def project(n):
             acc = banks.tile([P, HEADS_PER_ROUND, P], F32, tag="bank")
@@ -177,9 +197,6 @@ def tile_attention_pa_s_kernel(tc, query, wq_words, wq_scales, bq, cos, sin, out
 
         products = []
         for n in range(ROUNDS):
-            acc = project(n)
-            if n == 0:
-                flip_tables()
-            products.append(multiply(add_bias(n, acc)))
+            products.append(multiply(add_bias(n, project(n))))
         for n in range(ROUNDS):
             store(n, join(products[n][0], products[n][1]))

@@ -16,9 +16,11 @@ P = 128
 PACK = 4
 K_PASS = P * PACK
 PASSES = DIM // K_PASS
-HEADS_PER_ROUND = 4
-ROUNDS = H // HEADS_PER_ROUND
+GROUPS = (4, 4, 4, 2, 2)
+ROUNDS = len(GROUPS)
 PSUM_BANKS = 7
+
+IDLE_COLUMNS = 64
 
 FLOPS = 2 * B * S * DIM * E
 
@@ -77,9 +79,11 @@ def tile_attention_pa_s_kernel(tc, query, wq_words, wq_scales, bq, cos, sin, out
 
         def keep_busy(times):
             for i in range(times):
-                nc.tensor.matmul(out=idle_bank[:], lhsT=ident[:], rhs=ident[:], start=True, stop=True)
+                nc.tensor.matmul(
+                    out=idle_bank[:, 0:IDLE_COLUMNS], lhsT=ident[:], rhs=ident[:, 0:IDLE_COLUMNS], start=True, stop=True
+                )
 
-        keep_busy(3)
+        keep_busy(5)
 
         sign = keep.tile([P, 1], F32)
         nc.vector.memset(sign[0:HALF], 1.0)
@@ -110,9 +114,6 @@ def tile_attention_pa_s_kernel(tc, query, wq_words, wq_scales, bq, cos, sin, out
             nc.vector.quantize_mx(out=x_codes[:, g, :].bitcast(FP8X4), scales=x_planes[:, g, :], in_=grouped[:, g, :])
 
         tables = keep.tile([P, 2, P], BF16)
-        by_head = [P, HEADS_PER_ROUND, P]
-        cos_by_head = tables[:, 0, :].unsqueeze(1).to_broadcast(by_head)
-        sin_by_head = tables[:, 1, :].unsqueeze(1).to_broadcast(by_head)
 
         def flip_tables():
             tables_flipped = banks.tile([P, 2, P], BF16, tag="bank")
@@ -136,10 +137,10 @@ def tile_attention_pa_s_kernel(tc, query, wq_words, wq_scales, bq, cos, sin, out
 
         keep_busy(3)
 
-        def project(n):
-            acc = banks.tile([P, HEADS_PER_ROUND, P], F32, tag="bank")
-            for j in range(HEADS_PER_ROUND):
-                h = n * HEADS_PER_ROUND + j
+        def project(first, count):
+            acc = banks.tile([P, count, P], F32, tag="bank")
+            for j in range(count):
+                h = first + j
                 for g in range(PASSES):
                     nc.tensor.matmul_mx(
                         out=acc[:, j, :],
@@ -152,10 +153,10 @@ def tile_attention_pa_s_kernel(tc, query, wq_words, wq_scales, bq, cos, sin, out
                     )
             return acc
 
-        def add_bias(n, acc):
-            q_sb = rounds.tile([P, HEADS_PER_ROUND, P], F32)
-            for j in range(HEADS_PER_ROUND):
-                h = n * HEADS_PER_ROUND + j
+        def add_bias(first, count, acc):
+            q_sb = rounds.tile([P, count, P], F32, tag="q_sb")
+            for j in range(count):
+                h = first + j
                 nc.scalar.activation(
                     out=q_sb[:, j, :],
                     in_=acc[:, j, :],
@@ -165,16 +166,21 @@ def tile_attention_pa_s_kernel(tc, query, wq_words, wq_scales, bq, cos, sin, out
                 )
             return q_sb
 
-        def multiply(q_sb):
-            by_cos = rounds.tile([P, HEADS_PER_ROUND, P], F32)
-            nc.vector.tensor_tensor(out=by_cos[:], in0=q_sb[:], in1=cos_by_head, op=mybir.AluOpType.mult)
-            by_sin = rounds.tile([P, HEADS_PER_ROUND, P], F32)
-            nc.vector.tensor_tensor(out=by_sin[:], in0=q_sb[:], in1=sin_by_head, op=mybir.AluOpType.mult)
+        def multiply(count, q_sb):
+            by_head = [P, count, P]
+            by_cos = rounds.tile(by_head, F32, tag="by_cos")
+            nc.vector.tensor_tensor(
+                out=by_cos[:], in0=q_sb[:], in1=tables[:, 0, :].unsqueeze(1).to_broadcast(by_head), op=mybir.AluOpType.mult
+            )
+            by_sin = rounds.tile(by_head, F32, tag="by_sin")
+            nc.vector.tensor_tensor(
+                out=by_sin[:], in0=q_sb[:], in1=tables[:, 1, :].unsqueeze(1).to_broadcast(by_head), op=mybir.AluOpType.mult
+            )
             return by_cos, by_sin
 
-        def join(by_cos, by_sin):
-            joined = banks.tile([P, HEADS_PER_ROUND, HD], F32, tag="bank")
-            for j in range(HEADS_PER_ROUND):
+        def join(count, by_cos, by_sin):
+            joined = banks.tile([P, count, HD], F32, tag="bank")
+            for j in range(count):
                 nc.tensor.matmul(
                     out=joined[:, j, :], lhsT=by_cos[:, j, :], rhs=ident[:], is_transpose=True, start=True, stop=False
                 )
@@ -188,15 +194,18 @@ def tile_attention_pa_s_kernel(tc, query, wq_words, wq_scales, bq, cos, sin, out
                 )
             return joined
 
-        def store(n, joined):
-            out_sb = rounds.tile([P, HEADS_PER_ROUND, HD], F32)
-            nc.scalar.copy(out=out_sb[:], in_=joined[:])
-            heads = slice(n * HEADS_PER_ROUND, (n + 1) * HEADS_PER_ROUND)
+        def store(first, count, joined, on_vector):
+            out_sb = rounds.tile([P, count, HD], F32, tag="out_sb")
+            if on_vector:
+                nc.vector.tensor_copy(out=out_sb[:], in_=joined[:])
+            else:
+                nc.scalar.copy(out=out_sb[:], in_=joined[:])
             for b in range(B):
-                nc.sync.dma_start(out=out[b, heads].rearrange("h s d -> s h d"), in_=out_sb[b:P:B])
+                nc.sync.dma_start(out=out[b, first : first + count].rearrange("h s d -> s h d"), in_=out_sb[b:P:B])
 
+        firsts = [sum(GROUPS[:i]) for i in range(len(GROUPS))]
         products = []
-        for n in range(ROUNDS):
-            products.append(multiply(add_bias(n, project(n))))
-        for n in range(ROUNDS):
-            store(n, join(products[n][0], products[n][1]))
+        for first, count in zip(firsts, GROUPS):
+            products.append(multiply(count, add_bias(first, count, project(first, count))))
+        for i, (first, count) in enumerate(zip(firsts, GROUPS)):
+            store(first, count, join(count, products[i][0], products[i][1]), i == len(GROUPS) - 2)

@@ -17,7 +17,8 @@ PACK = 4
 K_PASS = P * PACK
 PASSES = DIM // K_PASS
 GROUPS = (4, 4, 4, 2, 2)
-ROUNDS = len(GROUPS)
+PRODUCT_GROUPS = ((3, False), (1, True), (3, False), (1, True), (3, False), (1, True), (2, False), (2, False))
+ROUNDS = len(PRODUCT_GROUPS)
 PSUM_BANKS = 7
 
 IDLE_COLUMNS = 64
@@ -153,40 +154,51 @@ def tile_attention_pa_s_kernel(tc, query, wq_words, wq_scales, bq, cos, sin, out
                     )
             return acc
 
-        def add_bias(first, count, acc):
-            q_sb = rounds.tile([P, count, P], F32, tag="q_sb")
+        by_cos = {}
+        by_sin = {}
+
+        def multiply_on_vector(first, count, acc):
+            cos_part = rounds.tile([P, count, P], F32, tag="cos_part")
+            sin_part = rounds.tile([P, count, P], F32, tag="sin_part")
             for j in range(count):
                 h = first + j
-                nc.scalar.activation(
-                    out=q_sb[:, j, :],
-                    in_=acc[:, j, :],
-                    func=mybir.ActivationFunctionType.Identity,
-                    bias=bias_col[:, h : h + 1],
-                    scale=1.0,
-                )
-            return q_sb
+                for part, table in ((cos_part, 0), (sin_part, 1)):
+                    nc.vector.scalar_tensor_tensor(
+                        out=part[:, j, :],
+                        in0=acc[:, j, :],
+                        scalar=bias_col[:, h : h + 1],
+                        in1=tables[:, table, :],
+                        op0=mybir.AluOpType.add,
+                        op1=mybir.AluOpType.mult,
+                    )
+                by_cos[h] = cos_part[:, j, :]
+                by_sin[h] = sin_part[:, j, :]
 
-        def multiply(count, q_sb):
-            by_head = [P, count, P]
-            by_cos = rounds.tile(by_head, F32, tag="by_cos")
-            nc.vector.tensor_tensor(
-                out=by_cos[:], in0=q_sb[:], in1=tables[:, 0, :].unsqueeze(1).to_broadcast(by_head), op=mybir.AluOpType.mult
+        def multiply_on_gpsimd(h, acc):
+            q_sb = rounds.tile([P, P], F32, tag="q_sb")
+            nc.scalar.activation(
+                out=q_sb[:],
+                in_=acc[:, 0, :],
+                func=mybir.ActivationFunctionType.Identity,
+                bias=bias_col[:, h : h + 1],
+                scale=1.0,
             )
-            by_sin = rounds.tile(by_head, F32, tag="by_sin")
-            nc.vector.tensor_tensor(
-                out=by_sin[:], in0=q_sb[:], in1=tables[:, 1, :].unsqueeze(1).to_broadcast(by_head), op=mybir.AluOpType.mult
-            )
-            return by_cos, by_sin
+            cos_one = rounds.tile([P, P], F32, tag="cos_one")
+            nc.gpsimd.tensor_tensor(out=cos_one[:], in0=q_sb[:], in1=tables[:, 0, :], op=mybir.AluOpType.mult)
+            sin_one = rounds.tile([P, P], F32, tag="sin_one")
+            nc.gpsimd.tensor_tensor(out=sin_one[:], in0=q_sb[:], in1=tables[:, 1, :], op=mybir.AluOpType.mult)
+            by_cos[h] = cos_one[:]
+            by_sin[h] = sin_one[:]
 
-        def join(count, by_cos, by_sin):
+        def join(first, count):
             joined = banks.tile([P, count, HD], F32, tag="bank")
             for j in range(count):
                 nc.tensor.matmul(
-                    out=joined[:, j, :], lhsT=by_cos[:, j, :], rhs=ident[:], is_transpose=True, start=True, stop=False
+                    out=joined[:, j, :], lhsT=by_cos[first + j], rhs=ident[:], is_transpose=True, start=True, stop=False
                 )
                 nc.tensor.matmul(
                     out=joined[:, j, :],
-                    lhsT=by_sin[:, j, :],
+                    lhsT=by_sin[first + j],
                     rhs=swap[:].rearrange("p f j -> p (f j)"),
                     is_transpose=True,
                     start=False,
@@ -203,9 +215,15 @@ def tile_attention_pa_s_kernel(tc, query, wq_words, wq_scales, bq, cos, sin, out
             for b in range(B):
                 nc.sync.dma_start(out=out[b, first : first + count].rearrange("h s d -> s h d"), in_=out_sb[b:P:B])
 
-        firsts = [sum(GROUPS[:i]) for i in range(len(GROUPS))]
-        products = []
-        for first, count in zip(firsts, GROUPS):
-            products.append(multiply(count, add_bias(first, count, project(first, count))))
-        for i, (first, count) in enumerate(zip(firsts, GROUPS)):
-            store(first, count, join(count, products[i][0], products[i][1]), i == len(GROUPS) - 2)
+        first = 0
+        for count, on_gpsimd in PRODUCT_GROUPS:
+            acc = project(first, count)
+            if on_gpsimd:
+                multiply_on_gpsimd(first, acc)
+            else:
+                multiply_on_vector(first, count, acc)
+            first += count
+        first = 0
+        for i, count in enumerate(GROUPS):
+            store(first, count, join(first, count), i == len(GROUPS) - 2)
+            first += count

@@ -21,6 +21,9 @@ PRODUCT_GROUPS = ((3, False), (1, True), (3, False), (1, True), (3, False), (1, 
 ROUNDS = len(PRODUCT_GROUPS)
 PSUM_BANKS = 7
 
+W_LOADS = 4
+W_LOAD_HEADS = H // W_LOADS
+W_LOAD_BYTES = 2 * E // W_LOADS
 IDLE_COLUMNS = 64
 
 FLOPS = 2 * B * S * DIM * E
@@ -52,24 +55,28 @@ def tile_attention_pa_s_kernel(tc, query, wq_words, wq_scales, bq, cos, sin, out
         w_planes = keep.tile([P, PASSES, E], U8, align_bytes=64)
         nc.vector.memset(w_planes[:].bitcast(I32), 0)
         scale_rows = wq_scales.rearrange("g (q r) n -> r q g n", r=PACK)
-        w_words = keep.tile([P, PASSES, 2 * E], U8, align_bytes=64)
-        words_by_partition = wq_words.rearrange("g p c -> p g c")
 
         def load_scales(r):
             nc.sync.dma_start(out=w_planes[r:P:32, :, :].bitcast(I32), in_=scale_rows[r].bitcast(I32))
 
-        def load_words(half):
-            byte_cols = slice(half * E, (half + 1) * E)
+        words_by_partition = wq_words.rearrange("g p c -> p g c")
+        w_words = []
+
+        def load_words(n):
+            chunk = keep.tile([P, PASSES, W_LOAD_BYTES], U8, align_bytes=64, name="w_words_%d" % n)
             nc.sync.dma_start(
-                out=w_words[:, :, byte_cols].bitcast(I32), in_=words_by_partition[:, :, byte_cols].bitcast(I32)
+                out=chunk[:].bitcast(I32),
+                in_=words_by_partition[:, :, n * W_LOAD_BYTES : (n + 1) * W_LOAD_BYTES].bitcast(I32),
             )
+            w_words.append(chunk)
 
         load_scales(0)
         load_scales(1)
         load_scales(2)
         load_words(0)
         load_scales(3)
-        load_words(1)
+        for n in range(1, W_LOADS):
+            load_words(n)
 
         warm = keep.tile([P, 2], F32)
         nc.gpsimd.memset(warm[:], 0.0)
@@ -84,7 +91,7 @@ def tile_attention_pa_s_kernel(tc, query, wq_words, wq_scales, bq, cos, sin, out
                     out=idle_bank[:, 0:IDLE_COLUMNS], lhsT=ident[:], rhs=ident[:, 0:IDLE_COLUMNS], start=True, stop=True
                 )
 
-        keep_busy(5)
+        keep_busy(3)
 
         sign = keep.tile([P, 1], F32)
         nc.vector.memset(sign[0:HALF], 1.0)
@@ -145,7 +152,9 @@ def tile_attention_pa_s_kernel(tc, query, wq_words, wq_scales, bq, cos, sin, out
                 for g in range(PASSES):
                     nc.tensor.matmul_mx(
                         out=acc[:, j, :],
-                        lhsT=w_words[:, g, 2 * h * HD : 2 * (h + 1) * HD].bitcast(FP4X4),
+                        lhsT=w_words[h // W_LOAD_HEADS][
+                            :, g, 2 * (h % W_LOAD_HEADS) * HD : 2 * (h % W_LOAD_HEADS + 1) * HD
+                        ].bitcast(FP4X4),
                         lhsT_scale=w_planes[:, g, h * HD : (h + 1) * HD],
                         rhs=x_codes[:, g, :].bitcast(FP8X4),
                         rhs_scale=x_planes[:, g, :],

@@ -16,8 +16,8 @@ P = 128
 PACK = 4
 K_PASS = P * PACK
 PASSES = DIM // K_PASS
-GROUPS = (4, 4, 4, 2, 2)
-PRODUCT_GROUPS = ((3, False), (1, True), (3, False), (1, True), (3, False), (1, True), (2, False), (2, False))
+GROUPS = (4, 4, 4, 2, 1, 1)
+PRODUCT_GROUPS = ((1, True), (3, False), (1, True), (3, False), (1, True), (3, False), (1, True), (3, False))
 ROUNDS = len(PRODUCT_GROUPS)
 PSUM_BANKS = 7
 
@@ -165,23 +165,22 @@ def tile_attention_pa_s_kernel(tc, query, wq_words, wq_scales, bq, cos, sin, out
 
         by_cos = {}
         by_sin = {}
+        twice = [P, 2, P]
 
         def multiply_on_vector(first, count, acc):
-            cos_part = rounds.tile([P, count, P], F32, tag="cos_part")
-            sin_part = rounds.tile([P, count, P], F32, tag="sin_part")
+            parts = rounds.tile([P, count, 2, P], F32, tag="parts")
             for j in range(count):
                 h = first + j
-                for part, table in ((cos_part, 0), (sin_part, 1)):
-                    nc.vector.scalar_tensor_tensor(
-                        out=part[:, j, :],
-                        in0=acc[:, j, :],
-                        scalar=bias_col[:, h : h + 1],
-                        in1=tables[:, table, :],
-                        op0=mybir.AluOpType.add,
-                        op1=mybir.AluOpType.mult,
-                    )
-                by_cos[h] = cos_part[:, j, :]
-                by_sin[h] = sin_part[:, j, :]
+                nc.vector.scalar_tensor_tensor(
+                    out=parts[:, j, :, :],
+                    in0=acc[:, j, :].unsqueeze(1).to_broadcast(twice),
+                    scalar=bias_col[:, h : h + 1],
+                    in1=tables[:],
+                    op0=mybir.AluOpType.add,
+                    op1=mybir.AluOpType.mult,
+                )
+                by_cos[h] = parts[:, j, 0, :]
+                by_sin[h] = parts[:, j, 1, :]
 
         def multiply_on_gpsimd(h, acc):
             q_sb = rounds.tile([P, P], F32, tag="q_sb")
@@ -192,12 +191,12 @@ def tile_attention_pa_s_kernel(tc, query, wq_words, wq_scales, bq, cos, sin, out
                 bias=bias_col[:, h : h + 1],
                 scale=1.0,
             )
-            cos_one = rounds.tile([P, P], F32, tag="cos_one")
-            nc.gpsimd.tensor_tensor(out=cos_one[:], in0=q_sb[:], in1=tables[:, 0, :], op=mybir.AluOpType.mult)
-            sin_one = rounds.tile([P, P], F32, tag="sin_one")
-            nc.gpsimd.tensor_tensor(out=sin_one[:], in0=q_sb[:], in1=tables[:, 1, :], op=mybir.AluOpType.mult)
-            by_cos[h] = cos_one[:]
-            by_sin[h] = sin_one[:]
+            pair = rounds.tile(twice, F32, tag="pair")
+            nc.gpsimd.tensor_tensor(
+                out=pair[:], in0=q_sb[:].unsqueeze(1).to_broadcast(twice), in1=tables[:], op=mybir.AluOpType.mult
+            )
+            by_cos[h] = pair[:, 0, :]
+            by_sin[h] = pair[:, 1, :]
 
         def join(first, count):
             joined = banks.tile([P, count, HD], F32, tag="bank")

@@ -16,7 +16,7 @@ P = 128
 PACK = 4
 K_PASS = P * PACK
 PASSES = DIM // K_PASS
-GROUPS = (4, 4, 4, 2, 1, 1)
+GROUPS = (4, 4, 4, 3, 1)
 PRODUCT_GROUPS = ((1, True), (3, False), (1, True), (3, False), (1, True), (3, False), (1, True), (3, False))
 ROUNDS = len(PRODUCT_GROUPS)
 PSUM_BANKS = 7

@@ -233,5 +233,5 @@ def tile_attention_pa_s_kernel(tc, query, wq_words, wq_scales, bq, cos, sin, out
             first += count
         first = 0
         for i, count in enumerate(GROUPS):
-            store(first, count, join(first, count), i == len(GROUPS) - 2)
+            store(first, count, join(first, count), i == len(GROUPS) - 1)
             first += count

@@ -16,7 +16,7 @@ P = 128
 PACK = 4
 K_PASS = P * PACK
 PASSES = DIM // K_PASS
-GROUPS = (4, 4, 4, 3, 1)
+GROUPS = (4, 4, 4, 2, 2)
 PRODUCT_GROUPS = ((1, True), (3, False), (1, True), (3, False), (1, True), (3, False), (1, True), (3, False))
 ROUNDS = len(PRODUCT_GROUPS)
 PSUM_BANKS = 7

@@ -78,6 +78,8 @@ def tile_attention_pa_s_kernel(tc, query, wq_words, wq_scales, bq, cos, sin, out
         for n in range(1, W_LOADS):
             load_words(n)
 
+        idle_ones = keep.tile([P, P], F32)
+        nc.gpsimd.memset(idle_ones[:], 1.0)
         warm = keep.tile([P, 2], F32)
         nc.gpsimd.memset(warm[:], 0.0)
         ident = keep.tile([P, P], F32)
@@ -85,13 +87,14 @@ def tile_attention_pa_s_kernel(tc, query, wq_words, wq_scales, bq, cos, sin, out
 
         idle_bank = idle.tile([P, P], F32)
 
-        def keep_busy(times):
+        def keep_busy(times, columns):
             for i in range(times):
                 nc.tensor.matmul(
-                    out=idle_bank[:, 0:IDLE_COLUMNS], lhsT=ident[:], rhs=ident[:, 0:IDLE_COLUMNS], start=True, stop=True
+                    out=idle_bank[:, 0:columns], lhsT=idle_ones[:], rhs=idle_ones[:, 0:columns], start=True, stop=True
                 )
 
-        keep_busy(3)
+        keep_busy(2, P)
+        keep_busy(3, IDLE_COLUMNS)
 
         sign = keep.tile([P, 1], F32)
         nc.vector.memset(sign[0:HALF], 1.0)
@@ -143,7 +146,7 @@ def tile_attention_pa_s_kernel(tc, query, wq_words, wq_scales, bq, cos, sin, out
         bias_col = keep.tile([P, H], F32)
         nc.scalar.copy(out=bias_col[:], in_=bias_flipped[:, 0:H])
 
-        keep_busy(3)
+        keep_busy(3, IDLE_COLUMNS)
 
         def project(first, count):
             acc = banks.tile([P, count, P], F32, tag="bank")

@@ -16,9 +16,11 @@ P = 128
 PACK = 4
 K_PASS = P * PACK
 PASSES = DIM // K_PASS
-GROUPS = (4, 4, 4, 2, 2)
-PRODUCT_GROUPS = ((1, True), (3, False), (1, True), (3, False), (1, True), (3, False), (1, True), (3, False))
-ROUNDS = len(PRODUCT_GROUPS)
+JOINS = ((1,), (2,), (3,), (0,), (5,), (4,), (6,), (7,))
+PAIR = 2
+PAIRS = H // PAIR
+RUN = S * B // PAIR
+GPSIMD_PAIRS = (0, 4)
 PSUM_BANKS = 7
 
 W_LOADS = 4
@@ -31,7 +33,7 @@ FLOPS = 2 * B * S * DIM * E
 
 def tile_attention_pa_s_kernel(tc, query, wq_words, wq_scales, bq, cos, sin, out):
     nc = tc.nc
-    with tc.tile_pool(name="keep", bufs=1) as keep, tc.tile_pool(name="rounds", bufs=ROUNDS) as rounds, tc.psum_pool(
+    with tc.tile_pool(name="keep", bufs=1) as keep, tc.tile_pool(name="rounds", bufs=PAIRS) as rounds, tc.psum_pool(
         name="banks", bufs=PSUM_BANKS
     ) as banks, tc.psum_pool(name="idle", bufs=1) as idle, tc.manual_schedule():
 
@@ -104,17 +106,20 @@ def tile_attention_pa_s_kernel(tc, query, wq_words, wq_scales, bq, cos, sin, out
         swap = keep.tile([P, 2, HALF], F32)
         for f in range(2):
             nc.vector.tensor_copy(out=swap[:, f, :], in_=ident[:, (1 - f) * HALF : (2 - f) * HALF])
+        regroup = keep.tile([P, PAIR, S // PAIR, B], F32)
+        nc.vector.tensor_copy(out=regroup[:], in_=ident[:].rearrange("p (m t b) -> p t m b", t=PAIR, b=B))
 
         nc.scalar.activation(out=warm[:, 1:2], in_=warm[:, 0:1], func=mybir.ActivationFunctionType.Identity)
 
         x_words = x_sb[:].bitcast(F32)
+        by_regroup = regroup[:].rearrange("p t m b -> p (t m b)")
         grouped = keep.tile([P, PASSES, P * PACK], BF16, align_bytes=64)
         x_codes = keep.tile([P, PASSES, P], U32, align_bytes=64)
         x_planes = keep.tile([P, PASSES, P], U8, align_bytes=64)
         for g in range(PASSES):
             flipped = banks.tile([P, 2, P], F32, tag="bank")
             for u in range(2):
-                nc.tensor.transpose(flipped[:, u, :], x_words[:, 256 * g + u : 256 * (g + 1) : 2], ident[:])
+                nc.tensor.transpose(flipped[:, u, :], x_words[:, 256 * g + u : 256 * (g + 1) : 2], by_regroup)
             pairs_out = grouped[:, g, :].bitcast(F32).rearrange("p (r u) -> p r u", u=2)
             pairs_in = flipped[:].rearrange("p u r -> p r u")
             if g % 2 == 0:
@@ -130,10 +135,13 @@ def tile_attention_pa_s_kernel(tc, query, wq_words, wq_scales, bq, cos, sin, out
             tables_flipped = banks.tile([P, 2, P], BF16, tag="bank")
             nc.tensor.transpose(tables_flipped[:, 0, :], cos_sb[:], ident_bf[:])
             nc.tensor.transpose(tables_flipped[:, 1, :], sin_twice[:, HALF : HALF + HD], ident_bf[:])
-            nc.vector.tensor_copy(out=tables[:, 0, :], in_=tables_flipped[:, 0, :])
+            nc.vector.tensor_copy(
+                out=tables[:, 0, :].rearrange("p (t m b) -> p t m b", t=PAIR, b=B),
+                in_=tables_flipped[:, 0, :].rearrange("p (m t b) -> p t m b", t=PAIR, b=B),
+            )
             nc.vector.tensor_scalar(
-                out=tables[:, 1, :],
-                in0=tables_flipped[:, 1, :],
+                out=tables[:, 1, :].rearrange("p (t m b) -> p t m b", t=PAIR, b=B),
+                in0=tables_flipped[:, 1, :].rearrange("p (m t b) -> p t m b", t=PAIR, b=B),
                 scalar1=sign[:, 0:1],
                 scalar2=None,
                 op0=mybir.AluOpType.mult,
@@ -166,75 +174,86 @@ def tile_attention_pa_s_kernel(tc, query, wq_words, wq_scales, bq, cos, sin, out
                     )
             return acc
 
-        by_cos = {}
-        by_sin = {}
-        twice = [P, 2, P]
+        products = []
+        whole = [P, 2, PAIR, RUN]
 
-        def multiply_on_vector(first, count, acc):
-            parts = rounds.tile([P, count, 2, P], F32, tag="parts")
-            for j in range(count):
-                h = first + j
+        def head_view(parts, j):
+            return parts[:, :, :, j, :]
+
+        def twice(sums):
+            return sums.rearrange("p (t r) -> p t r", t=PAIR).unsqueeze(1).to_broadcast(whole)
+
+        both_tables = tables[:].rearrange("p c (t r) -> p c t r", t=PAIR)
+
+        def multiply_on_vector(pair, acc):
+            parts = rounds.tile([P, 2, PAIR, PAIR, RUN], F32, tag="parts")
+            for j in range(PAIR):
+                h = PAIR * pair + j
                 nc.vector.scalar_tensor_tensor(
-                    out=parts[:, j, :, :],
-                    in0=acc[:, j, :].unsqueeze(1).to_broadcast(twice),
+                    out=head_view(parts, j),
+                    in0=twice(acc[:, j, :]),
                     scalar=bias_col[:, h : h + 1],
-                    in1=tables[:],
+                    in1=both_tables,
                     op0=mybir.AluOpType.add,
                     op1=mybir.AluOpType.mult,
                 )
-                by_cos[h] = parts[:, j, 0, :]
-                by_sin[h] = parts[:, j, 1, :]
+            products.append(parts)
 
-        def multiply_on_gpsimd(h, acc):
-            q_sb = rounds.tile([P, P], F32, tag="q_sb")
-            nc.scalar.activation(
-                out=q_sb[:],
-                in_=acc[:, 0, :],
-                func=mybir.ActivationFunctionType.Identity,
-                bias=bias_col[:, h : h + 1],
-                scale=1.0,
-            )
-            pair = rounds.tile(twice, F32, tag="pair")
-            nc.gpsimd.tensor_tensor(
-                out=pair[:], in0=q_sb[:].unsqueeze(1).to_broadcast(twice), in1=tables[:], op=mybir.AluOpType.mult
-            )
-            by_cos[h] = pair[:, 0, :]
-            by_sin[h] = pair[:, 1, :]
+        def multiply_on_gpsimd(pair, acc):
+            parts = rounds.tile([P, 2, PAIR, PAIR, RUN], F32, tag="parts")
+            for j in range(PAIR):
+                h = PAIR * pair + j
+                q_sb = rounds.tile([P, P], F32, tag="q_sb")
+                nc.scalar.activation(
+                    out=q_sb[:],
+                    in_=acc[:, j, :],
+                    func=mybir.ActivationFunctionType.Identity,
+                    bias=bias_col[:, h : h + 1],
+                    scale=1.0,
+                )
+                nc.gpsimd.tensor_tensor(
+                    out=head_view(parts, j), in0=twice(q_sb[:]), in1=both_tables, op=mybir.AluOpType.mult
+                )
+            products.append(parts)
 
-        def join(first, count):
-            joined = banks.tile([P, count, HD], F32, tag="bank")
-            for j in range(count):
-                nc.tensor.matmul(
-                    out=joined[:, j, :], lhsT=by_cos[first + j], rhs=ident[:], is_transpose=True, start=True, stop=False
-                )
-                nc.tensor.matmul(
-                    out=joined[:, j, :],
-                    lhsT=by_sin[first + j],
-                    rhs=swap[:].rearrange("p f j -> p (f j)"),
-                    is_transpose=True,
-                    start=False,
-                    stop=True,
-                )
+        def join(pairs):
+            joined = banks.tile([P, len(pairs), PAIR, HD], F32, tag="bank")
+            for j, pair in enumerate(pairs):
+                parts = products[pair]
+                for t in range(PAIR):
+                    nc.tensor.matmul(
+                        out=joined[:, j, t, :],
+                        lhsT=parts[:, 0, t, :, :].rearrange("p h r -> p (h r)"),
+                        rhs=ident[:],
+                        is_transpose=True,
+                        start=True,
+                        stop=False,
+                    )
+                    nc.tensor.matmul(
+                        out=joined[:, j, t, :],
+                        lhsT=parts[:, 1, t, :, :].rearrange("p h r -> p (h r)"),
+                        rhs=swap[:].rearrange("p f j -> p (f j)"),
+                        is_transpose=True,
+                        start=False,
+                        stop=True,
+                    )
             return joined
 
-        def store(first, count, joined, on_vector):
-            out_sb = rounds.tile([P, count, HD], F32, tag="out_sb")
+        def store(pairs, joined, on_vector):
+            out_sb = rounds.tile([P, len(pairs), PAIR * HD], F32, tag="out_sb")
             if on_vector:
-                nc.vector.tensor_copy(out=out_sb[:], in_=joined[:])
+                nc.vector.tensor_copy(out=out_sb[:], in_=joined[:].rearrange("p c t d -> p c (t d)"))
             else:
-                nc.scalar.copy(out=out_sb[:], in_=joined[:])
-            for b in range(B):
-                nc.sync.dma_start(out=out[b, first : first + count].rearrange("h s d -> s h d"), in_=out_sb[b:P:B])
+                nc.scalar.copy(out=out_sb[:], in_=joined[:].rearrange("p c t d -> p c (t d)"))
+            for j, pair in enumerate(pairs):
+                heads = out[:, PAIR * pair : PAIR * (pair + 1)]
+                nc.sync.dma_start(out=heads.rearrange("b h (m t) d -> (h m) b (t d)", t=PAIR), in_=out_sb[:, j, :])
 
-        first = 0
-        for count, on_gpsimd in PRODUCT_GROUPS:
-            acc = project(first, count)
-            if on_gpsimd:
-                multiply_on_gpsimd(first, acc)
+        for pair in range(PAIRS):
+            acc = project(PAIR * pair, PAIR)
+            if pair in GPSIMD_PAIRS:
+                multiply_on_gpsimd(pair, acc)
             else:
-                multiply_on_vector(first, count, acc)
-            first += count
-        first = 0
-        for i, count in enumerate(GROUPS):
-            store(first, count, join(first, count), i == len(GROUPS) - 1)
-            first += count
+                multiply_on_vector(pair, acc)
+        for i, pairs in enumerate(JOINS):
+            store(pairs, join(pairs), i == len(JOINS) - 1)

@@ -16,7 +16,7 @@ P = 128
 PACK = 4
 K_PASS = P * PACK
 PASSES = DIM // K_PASS
-JOINS = ((1,), (2,), (3,), (0,), (5,), (4,), (6,), (7,))
+JOINS = (1, 2, 3, 0, 5, 4, 6, 7)
 PAIR = 2
 PAIRS = H // PAIR
 RUN = S * B // PAIR
@@ -26,7 +26,6 @@ PSUM_BANKS = 7
 W_LOADS = 4
 W_LOAD_HEADS = H // W_LOADS
 W_LOAD_BYTES = 2 * E // W_LOADS
-IDLE_COLUMNS = 64
 
 FLOPS = 2 * B * S * DIM * E
 
@@ -40,19 +39,17 @@ def tile_attention_pa_s_kernel(tc, query, wq_words, wq_scales, bq, cos, sin, out
         x_sb = keep.tile([P, DIM], BF16)
         nc.scalar.dma_start(out=x_sb[:], in_=query.rearrange("b s k -> s b k"))
 
-        bias_rows = keep.tile([P, HD], BF16)
+        idle_ones = keep.tile([P, P], F32)
+        nc.gpsimd.memset(idle_ones[:], 1.0)
+        cos_sin = keep.tile([P, 2 * HD], BF16)
+        nc.scalar.dma_start(out=cos_sin[0:S, HALF : HALF + HD], in_=cos.rearrange("a c s d -> (a c s) d"))
         nc.scalar.dma_start(
-            out=bias_rows[:], in_=bq.rearrange("(h d) -> h d", h=H).unsqueeze(0).to_broadcast([P // H, H, HD])
+            out=cos_sin[S:P, :], in_=sin.rearrange("a c s d -> (a c s) d").unsqueeze(1).to_broadcast([S, 2, HD])
         )
 
-        cos_sb = keep.tile([P, HD], BF16)
-        nc.scalar.dma_start(
-            out=cos_sb[:], in_=cos.rearrange("a c s d -> (a c s) d").unsqueeze(1).to_broadcast([S, B, HD])
-        )
-        sin_twice = keep.tile([P, 2 * HD], BF16)
-        nc.scalar.dma_start(
-            out=sin_twice[:], in_=sin.rearrange("a c s d -> (a c s) d").unsqueeze(1).to_broadcast([S, 2 * B, HD])
-        )
+        bias_rows = keep.tile([P, HD], BF16)
+        nc.gpsimd.memset(bias_rows[:], 0.0)
+        nc.scalar.dma_start(out=bias_rows[0:H, :], in_=bq.rearrange("(h d) -> h d", h=H))
 
         w_planes = keep.tile([P, PASSES, E], U8, align_bytes=64)
         nc.vector.memset(w_planes[:].bitcast(I32), 0)
@@ -80,8 +77,6 @@ def tile_attention_pa_s_kernel(tc, query, wq_words, wq_scales, bq, cos, sin, out
         for n in range(1, W_LOADS):
             load_words(n)
 
-        idle_ones = keep.tile([P, P], F32)
-        nc.gpsimd.memset(idle_ones[:], 1.0)
         warm = keep.tile([P, 2], F32)
         nc.gpsimd.memset(warm[:], 0.0)
         ident = keep.tile([P, P], F32)
@@ -89,14 +84,14 @@ def tile_attention_pa_s_kernel(tc, query, wq_words, wq_scales, bq, cos, sin, out
 
         idle_bank = idle.tile([P, P], F32)
 
-        def keep_busy(times, columns):
+        def keep_busy(times):
             for i in range(times):
-                nc.tensor.matmul(
-                    out=idle_bank[:, 0:columns], lhsT=idle_ones[:], rhs=idle_ones[:, 0:columns], start=True, stop=True
-                )
+                nc.tensor.matmul(out=idle_bank[:], lhsT=idle_ones[:], rhs=idle_ones[:], start=True, stop=True)
 
-        keep_busy(2, P)
-        keep_busy(3, IDLE_COLUMNS)
+        keep_busy(3)
+
+        regroup = keep.tile([P, PAIR, S // PAIR, B], F32)
+        nc.vector.tensor_copy(out=regroup[:], in_=ident[:].rearrange("p (m t b) -> p t m b", t=PAIR, b=B))
 
         sign = keep.tile([P, 1], F32)
         nc.vector.memset(sign[0:HALF], 1.0)
@@ -106,9 +101,6 @@ def tile_attention_pa_s_kernel(tc, query, wq_words, wq_scales, bq, cos, sin, out
         swap = keep.tile([P, 2, HALF], F32)
         for f in range(2):
             nc.vector.tensor_copy(out=swap[:, f, :], in_=ident[:, (1 - f) * HALF : (2 - f) * HALF])
-        regroup = keep.tile([P, PAIR, S // PAIR, B], F32)
-        nc.vector.tensor_copy(out=regroup[:], in_=ident[:].rearrange("p (m t b) -> p t m b", t=PAIR, b=B))
-
         nc.scalar.activation(out=warm[:, 1:2], in_=warm[:, 0:1], func=mybir.ActivationFunctionType.Identity)
 
         x_words = x_sb[:].bitcast(F32)
@@ -132,16 +124,18 @@ def tile_attention_pa_s_kernel(tc, query, wq_words, wq_scales, bq, cos, sin, out
         tables = keep.tile([P, 2, P], BF16)
 
         def flip_tables():
-            tables_flipped = banks.tile([P, 2, P], BF16, tag="bank")
-            nc.tensor.transpose(tables_flipped[:, 0, :], cos_sb[:], ident_bf[:])
-            nc.tensor.transpose(tables_flipped[:, 1, :], sin_twice[:, HALF : HALF + HD], ident_bf[:])
+            tables_flipped = banks.tile([P, 2, S], BF16, tag="bank")
+            nc.tensor.transpose(
+                tables_flipped[:].rearrange("p c s -> p (c s)"), cos_sin[:, HALF : HALF + HD], ident_bf[:]
+            )
+            by_token = [P, PAIR, S // PAIR, B]
             nc.vector.tensor_copy(
                 out=tables[:, 0, :].rearrange("p (t m b) -> p t m b", t=PAIR, b=B),
-                in_=tables_flipped[:, 0, :].rearrange("p (m t b) -> p t m b", t=PAIR, b=B),
+                in_=tables_flipped[:, 0, :].rearrange("p (m t) -> p t m", t=PAIR).unsqueeze(3).to_broadcast(by_token),
             )
             nc.vector.tensor_scalar(
                 out=tables[:, 1, :].rearrange("p (t m b) -> p t m b", t=PAIR, b=B),
-                in0=tables_flipped[:, 1, :].rearrange("p (m t b) -> p t m b", t=PAIR, b=B),
+                in0=tables_flipped[:, 1, :].rearrange("p (m t) -> p t m", t=PAIR).unsqueeze(3).to_broadcast(by_token),
                 scalar1=sign[:, 0:1],
                 scalar2=None,
                 op0=mybir.AluOpType.mult,
@@ -154,7 +148,7 @@ def tile_attention_pa_s_kernel(tc, query, wq_words, wq_scales, bq, cos, sin, out
         bias_col = keep.tile([P, H], F32)
         nc.scalar.copy(out=bias_col[:], in_=bias_flipped[:, 0:H])
 
-        keep_busy(3, IDLE_COLUMNS)
+        keep_busy(2)
 
         def project(first, count):
             acc = banks.tile([P, count, P], F32, tag="bank")
@@ -216,38 +210,30 @@ def tile_attention_pa_s_kernel(tc, query, wq_words, wq_scales, bq, cos, sin, out
                 )
             products.append(parts)
 
-        def join(pairs):
-            joined = banks.tile([P, len(pairs), PAIR, HD], F32, tag="bank")
-            for j, pair in enumerate(pairs):
-                parts = products[pair]
-                for t in range(PAIR):
-                    nc.tensor.matmul(
-                        out=joined[:, j, t, :],
-                        lhsT=parts[:, 0, t, :, :].rearrange("p h r -> p (h r)"),
-                        rhs=ident[:],
-                        is_transpose=True,
-                        start=True,
-                        stop=False,
-                    )
-                    nc.tensor.matmul(
-                        out=joined[:, j, t, :],
-                        lhsT=parts[:, 1, t, :, :].rearrange("p h r -> p (h r)"),
-                        rhs=swap[:].rearrange("p f j -> p (f j)"),
-                        is_transpose=True,
-                        start=False,
-                        stop=True,
-                    )
-            return joined
+        def join(pair, t, joined):
+            parts = products[pair]
+            nc.tensor.matmul(
+                out=joined,
+                lhsT=parts[:, 0, t, :, :].rearrange("p h r -> p (h r)"),
+                rhs=ident[:],
+                is_transpose=True,
+                start=True,
+                stop=False,
+            )
+            nc.tensor.matmul(
+                out=joined,
+                lhsT=parts[:, 1, t, :, :].rearrange("p h r -> p (h r)"),
+                rhs=swap[:].rearrange("p f j -> p (f j)"),
+                is_transpose=True,
+                start=False,
+                stop=True,
+            )
 
-        def store(pairs, joined, on_vector):
-            out_sb = rounds.tile([P, len(pairs), PAIR * HD], F32, tag="out_sb")
-            if on_vector:
-                nc.vector.tensor_copy(out=out_sb[:], in_=joined[:].rearrange("p c t d -> p c (t d)"))
-            else:
-                nc.scalar.copy(out=out_sb[:], in_=joined[:].rearrange("p c t d -> p c (t d)"))
-            for j, pair in enumerate(pairs):
-                heads = out[:, PAIR * pair : PAIR * (pair + 1)]
-                nc.sync.dma_start(out=heads.rearrange("b h (m t) d -> (h m) b (t d)", t=PAIR), in_=out_sb[:, j, :])
+        def store(pair, out_sb):
+            heads = out[:, PAIR * pair : PAIR * (pair + 1)]
+            nc.sync.dma_start(
+                out=heads.rearrange("b h (m t) d -> (h m) b (t d)", t=PAIR), in_=out_sb[:].rearrange("p t d -> p (t d)")
+            )
 
         for pair in range(PAIRS):
             acc = project(PAIR * pair, PAIR)
@@ -255,5 +241,21 @@ def tile_attention_pa_s_kernel(tc, query, wq_words, wq_scales, bq, cos, sin, out
                 multiply_on_gpsimd(pair, acc)
             else:
                 multiply_on_vector(pair, acc)
-        for i, pairs in enumerate(JOINS):
-            store(pairs, join(pairs), i == len(JOINS) - 1)
+        for pair in JOINS[:-1]:
+            out_sb = rounds.tile([P, PAIR, HD], F32, tag="out_sb")
+            joined = banks.tile([P, PAIR, HD], F32, tag="bank")
+            for t in range(PAIR):
+                join(pair, t, joined[:, t, :])
+            nc.scalar.copy(out=out_sb[:], in_=joined[:])
+            store(pair, out_sb)
+
+        pair = JOINS[-1]
+        out_sb = rounds.tile([P, PAIR, HD], F32, tag="out_sb")
+        for t in range(PAIR):
+            slot = banks.tile([P, HD], F32, tag="bank")
+            join(pair, t, slot[:])
+            if t == 0:
+                nc.scalar.copy(out=out_sb[:, t, :], in_=slot[:])
+            else:
+                nc.vector.tensor_copy(out=out_sb[:, t, :], in_=slot[:])
+        store(pair, out_sb)

@@ -36,20 +36,23 @@ def tile_attention_pa_s_kernel(tc, query, wq_words, wq_scales, bq, cos, sin, out
         name="banks", bufs=PSUM_BANKS
     ) as banks, tc.psum_pool(name="idle", bufs=1) as idle, tc.manual_schedule():
 
-        x_sb = keep.tile([P, DIM], BF16)
-        nc.scalar.dma_start(out=x_sb[:], in_=query.rearrange("b s k -> s b k"))
-
         idle_ones = keep.tile([P, P], F32)
         nc.gpsimd.memset(idle_ones[:], 1.0)
         cos_sin = keep.tile([P, 2 * HD], BF16)
-        nc.scalar.dma_start(out=cos_sin[0:S, HALF : HALF + HD], in_=cos.rearrange("a c s d -> (a c s) d"))
-        nc.scalar.dma_start(
+        nc.sync.dma_start(out=cos_sin[0:S, HALF : HALF + HD], in_=cos.rearrange("a c s d -> (a c s) d"))
+        nc.sync.dma_start(
             out=cos_sin[S:P, :], in_=sin.rearrange("a c s d -> (a c s) d").unsqueeze(1).to_broadcast([S, 2, HD])
         )
 
+        x_passes = []
+        for g in range(PASSES):
+            x_sb = keep.tile([P, K_PASS], BF16, name="x_sb_%d" % g)
+            nc.scalar.dma_start(out=x_sb[:], in_=query[:, :, g * K_PASS : (g + 1) * K_PASS].rearrange("b s k -> s b k"))
+            x_passes.append(x_sb)
+
         bias_rows = keep.tile([P, HD], BF16)
         nc.gpsimd.memset(bias_rows[:], 0.0)
-        nc.scalar.dma_start(out=bias_rows[0:H, :], in_=bq.rearrange("(h d) -> h d", h=H))
+        nc.sync.dma_start(out=bias_rows[0:H, :], in_=bq.rearrange("(h d) -> h d", h=H))
 
         w_planes = keep.tile([P, PASSES, E], U8, align_bytes=64)
         nc.vector.memset(w_planes[:].bitcast(I32), 0)
@@ -71,8 +74,8 @@ def tile_attention_pa_s_kernel(tc, query, wq_words, wq_scales, bq, cos, sin, out
 
         load_scales(0)
         load_scales(1)
-        load_scales(2)
         load_words(0)
+        load_scales(2)
         load_scales(3)
         for n in range(1, W_LOADS):
             load_words(n)
@@ -103,15 +106,15 @@ def tile_attention_pa_s_kernel(tc, query, wq_words, wq_scales, bq, cos, sin, out
             nc.vector.tensor_copy(out=swap[:, f, :], in_=ident[:, (1 - f) * HALF : (2 - f) * HALF])
         nc.scalar.activation(out=warm[:, 1:2], in_=warm[:, 0:1], func=mybir.ActivationFunctionType.Identity)
 
-        x_words = x_sb[:].bitcast(F32)
         by_regroup = regroup[:].rearrange("p t m b -> p (t m b)")
         grouped = keep.tile([P, PASSES, P * PACK], BF16, align_bytes=64)
         x_codes = keep.tile([P, PASSES, P], U32, align_bytes=64)
         x_planes = keep.tile([P, PASSES, P], U8, align_bytes=64)
         for g in range(PASSES):
             flipped = banks.tile([P, 2, P], F32, tag="bank")
+            x_words = x_passes[g][:].bitcast(F32)
             for u in range(2):
-                nc.tensor.transpose(flipped[:, u, :], x_words[:, 256 * g + u : 256 * (g + 1) : 2], by_regroup)
+                nc.tensor.transpose(flipped[:, u, :], x_words[:, u : K_PASS // 2 : 2], by_regroup)
             pairs_out = grouped[:, g, :].bitcast(F32).rearrange("p (r u) -> p r u", u=2)
             pairs_in = flipped[:].rearrange("p u r -> p r u")
             if g % 2 == 0:

@@ -50,12 +50,12 @@ def tile_attention_pa_s_kernel(tc, query, wq_words, wq_scales, bq, cos, sin, out
             nc.scalar.dma_start(out=x_sb[:], in_=query[:, :, g * K_PASS : (g + 1) * K_PASS].rearrange("b s k -> s b k"))
             x_passes.append(x_sb)
 
-        bias_rows = keep.tile([P, HD], BF16)
-        nc.gpsimd.memset(bias_rows[:], 0.0)
-        nc.sync.dma_start(out=bias_rows[0:H, :], in_=bq.rearrange("(h d) -> h d", h=H))
-
         w_planes = keep.tile([P, PASSES, E], U8, align_bytes=64)
         nc.vector.memset(w_planes[:].bitcast(I32), 0)
+
+        bias_rows = keep.tile([P, HD], BF16)
+        nc.vector.memset(bias_rows[:], 0.0)
+
         scale_rows = wq_scales.rearrange("g (q r) n -> r q g n", r=PACK)
 
         def load_scales(r):
@@ -75,13 +75,12 @@ def tile_attention_pa_s_kernel(tc, query, wq_words, wq_scales, bq, cos, sin, out
         load_scales(0)
         load_scales(1)
         load_words(0)
+        nc.sync.dma_start(out=bias_rows[0:H, :], in_=bq.rearrange("(h d) -> h d", h=H))
         load_scales(2)
         load_scales(3)
         for n in range(1, W_LOADS):
             load_words(n)
 
-        warm = keep.tile([P, 2], F32)
-        nc.gpsimd.memset(warm[:], 0.0)
         ident = keep.tile([P, P], F32)
         make_identity(nc, ident[:])
 
@@ -104,7 +103,8 @@ def tile_attention_pa_s_kernel(tc, query, wq_words, wq_scales, bq, cos, sin, out
         swap = keep.tile([P, 2, HALF], F32)
         for f in range(2):
             nc.vector.tensor_copy(out=swap[:, f, :], in_=ident[:, (1 - f) * HALF : (2 - f) * HALF])
-        nc.scalar.activation(out=warm[:, 1:2], in_=warm[:, 0:1], func=mybir.ActivationFunctionType.Identity)
+        warm = keep.tile([P, 1], F32)
+        nc.scalar.activation(out=warm[:], in_=idle_ones[:, 0:1], func=mybir.ActivationFunctionType.Identity)
 
         by_regroup = regroup[:].rearrange("p t m b -> p (t m b)")
         grouped = keep.tile([P, PASSES, P * PACK], BF16, align_bytes=64)
@@ -249,7 +249,10 @@ def tile_attention_pa_s_kernel(tc, query, wq_words, wq_scales, bq, cos, sin, out
             joined = banks.tile([P, PAIR, HD], F32, tag="bank")
             for t in range(PAIR):
                 join(pair, t, joined[:, t, :])
-            nc.scalar.copy(out=out_sb[:], in_=joined[:])
+            if pair == JOINS[-2]:
+                nc.vector.tensor_copy(out=out_sb[:], in_=joined[:])
+            else:
+                nc.scalar.copy(out=out_sb[:], in_=joined[:])
             store(pair, out_sb)
 
         pair = JOINS[-1]

@@ -1,5 +1,4 @@
 import concourse.mybir as mybir
-from concourse.masks import make_identity
 
 F32 = mybir.dt.float32
 BF16 = mybir.dt.bfloat16
@@ -38,6 +37,16 @@ def tile_attention_pa_s_kernel(tc, query, wq_words, wq_scales, bq, cos, sin, out
 
         idle_ones = keep.tile([P, P], F32)
         nc.gpsimd.memset(idle_ones[:], 1.0)
+        ident = keep.tile([P, P], F32)
+        nc.gpsimd.affine_select(
+            out=ident[:],
+            in_=idle_ones[:],
+            pattern=[[-1, P]],
+            compare_op=mybir.AluOpType.is_equal,
+            fill=0.0,
+            base=0,
+            channel_multiplier=1,
+        )
         cos_sin = keep.tile([P, 2 * HD], BF16)
         nc.sync.dma_start(out=cos_sin[0:S, HALF : HALF + HD], in_=cos.rearrange("a c s d -> (a c s) d"))
         nc.sync.dma_start(
@@ -74,15 +83,12 @@ def tile_attention_pa_s_kernel(tc, query, wq_words, wq_scales, bq, cos, sin, out
 
         load_scales(0)
         load_scales(1)
-        load_words(0)
         nc.sync.dma_start(out=bias_rows[0:H, :], in_=bq.rearrange("(h d) -> h d", h=H))
+        load_words(0)
         load_scales(2)
         load_scales(3)
         for n in range(1, W_LOADS):
             load_words(n)
-
-        ident = keep.tile([P, P], F32)
-        make_identity(nc, ident[:])
 
         idle_bank = idle.tile([P, P], F32)
 

import concourse.mybir as mybir

F32 = mybir.dt.float32
BF16 = mybir.dt.bfloat16
I32 = mybir.dt.int32
U32 = mybir.dt.uint32
U8 = mybir.dt.uint8
FP8X4 = mybir.dt.float8_e4m3fn_x4
FP4X4 = mybir.dt.float4_e2m1fn_x4

B, S, DIM, H, HD = 2, 64, 1024, 16, 128
E = H * HD
HALF = HD // 2
P = 128
PACK = 4
K_PASS = P * PACK
PASSES = DIM // K_PASS
JOINS = (1, 2, 3, 0, 5, 4, 6, 7)
PAIR = 2
PAIRS = H // PAIR
RUN = S * B // PAIR
GPSIMD_PAIRS = (0, 4)
PSUM_BANKS = 7

W_LOADS = 4
W_LOAD_HEADS = H // W_LOADS
W_LOAD_BYTES = 2 * E // W_LOADS

FLOPS = 2 * B * S * DIM * E


def tile_attention_pa_s_kernel(tc, query, wq_words, wq_scales, bq, cos, sin, out):
    nc = tc.nc
    with tc.tile_pool(name="keep", bufs=1) as keep, tc.tile_pool(name="rounds", bufs=PAIRS) as rounds, tc.psum_pool(
        name="banks", bufs=PSUM_BANKS
    ) as banks, tc.psum_pool(name="idle", bufs=1) as idle, tc.manual_schedule():

        idle_ones = keep.tile([P, P], F32)
        nc.gpsimd.memset(idle_ones[:], 1.0)
        ident = keep.tile([P, P], F32)
        nc.gpsimd.affine_select(
            out=ident[:],
            in_=idle_ones[:],
            pattern=[[-1, P]],
            compare_op=mybir.AluOpType.is_equal,
            fill=0.0,
            base=0,
            channel_multiplier=1,
        )
        cos_sin = keep.tile([P, 2 * HD], BF16)
        nc.sync.dma_start(out=cos_sin[0:S, HALF : HALF + HD], in_=cos.rearrange("a c s d -> (a c s) d"))
        nc.sync.dma_start(
            out=cos_sin[S:P, :], in_=sin.rearrange("a c s d -> (a c s) d").unsqueeze(1).to_broadcast([S, 2, HD])
        )

        x_passes = []
        for g in range(PASSES):
            x_sb = keep.tile([P, K_PASS], BF16, name="x_sb_%d" % g)
            nc.scalar.dma_start(out=x_sb[:], in_=query[:, :, g * K_PASS : (g + 1) * K_PASS].rearrange("b s k -> s b k"))
            x_passes.append(x_sb)

        w_planes = keep.tile([P, PASSES, E], U8, align_bytes=64)
        nc.vector.memset(w_planes[:].bitcast(I32), 0)

        bias_rows = keep.tile([P, HD], BF16)
        nc.vector.memset(bias_rows[:], 0.0)

        scale_rows = wq_scales.rearrange("g (q r) n -> r q g n", r=PACK)

        def load_scales(r):
            nc.sync.dma_start(out=w_planes[r:P:32, :, :].bitcast(I32), in_=scale_rows[r].bitcast(I32))

        words_by_partition = wq_words.rearrange("g p c -> p g c")
        w_words = []

        def load_words(n):
            chunk = keep.tile([P, PASSES, W_LOAD_BYTES], U8, align_bytes=64, name="w_words_%d" % n)
            nc.sync.dma_start(
                out=chunk[:].bitcast(I32),
                in_=words_by_partition[:, :, n * W_LOAD_BYTES : (n + 1) * W_LOAD_BYTES].bitcast(I32),
            )
            w_words.append(chunk)

        load_scales(0)
        load_scales(1)
        nc.sync.dma_start(out=bias_rows[0:H, :], in_=bq.rearrange("(h d) -> h d", h=H))
        load_words(0)
        load_scales(2)
        load_scales(3)
        for n in range(1, W_LOADS):
            load_words(n)

        idle_bank = idle.tile([P, P], F32)

        def keep_busy(times):
            for i in range(times):
                nc.tensor.matmul(out=idle_bank[:], lhsT=idle_ones[:], rhs=idle_ones[:], start=True, stop=True)

        keep_busy(3)

        regroup = keep.tile([P, PAIR, S // PAIR, B], F32)
        nc.vector.tensor_copy(out=regroup[:], in_=ident[:].rearrange("p (m t b) -> p t m b", t=PAIR, b=B))

        sign = keep.tile([P, 1], F32)
        nc.vector.memset(sign[0:HALF], 1.0)
        nc.vector.memset(sign[HALF:P], -1.0)
        ident_bf = keep.tile([P, P], BF16)
        nc.vector.tensor_copy(out=ident_bf[:], in_=ident[:])
        swap = keep.tile([P, 2, HALF], F32)
        for f in range(2):
            nc.vector.tensor_copy(out=swap[:, f, :], in_=ident[:, (1 - f) * HALF : (2 - f) * HALF])
        warm = keep.tile([P, 1], F32)
        nc.scalar.activation(out=warm[:], in_=idle_ones[:, 0:1], func=mybir.ActivationFunctionType.Identity)

        by_regroup = regroup[:].rearrange("p t m b -> p (t m b)")
        grouped = keep.tile([P, PASSES, P * PACK], BF16, align_bytes=64)
        x_codes = keep.tile([P, PASSES, P], U32, align_bytes=64)
        x_planes = keep.tile([P, PASSES, P], U8, align_bytes=64)
        for g in range(PASSES):
            flipped = banks.tile([P, 2, P], F32, tag="bank")
            x_words = x_passes[g][:].bitcast(F32)
            for u in range(2):
                nc.tensor.transpose(flipped[:, u, :], x_words[:, u : K_PASS // 2 : 2], by_regroup)
            pairs_out = grouped[:, g, :].bitcast(F32).rearrange("p (r u) -> p r u", u=2)
            pairs_in = flipped[:].rearrange("p u r -> p r u")
            if g % 2 == 0:
                nc.vector.tensor_copy(out=pairs_out, in_=pairs_in)
            else:
                nc.scalar.copy(out=pairs_out, in_=pairs_in)
        for g in range(PASSES):
            nc.vector.quantize_mx(out=x_codes[:, g, :].bitcast(FP8X4), scales=x_planes[:, g, :], in_=grouped[:, g, :])

        tables = keep.tile([P, 2, P], BF16)

        def flip_tables():
            tables_flipped = banks.tile([P, 2, S], BF16, tag="bank")
            nc.tensor.transpose(
                tables_flipped[:].rearrange("p c s -> p (c s)"), cos_sin[:, HALF : HALF + HD], ident_bf[:]
            )
            by_token = [P, PAIR, S // PAIR, B]
            nc.vector.tensor_copy(
                out=tables[:, 0, :].rearrange("p (t m b) -> p t m b", t=PAIR, b=B),
                in_=tables_flipped[:, 0, :].rearrange("p (m t) -> p t m", t=PAIR).unsqueeze(3).to_broadcast(by_token),
            )
            nc.vector.tensor_scalar(
                out=tables[:, 1, :].rearrange("p (t m b) -> p t m b", t=PAIR, b=B),
                in0=tables_flipped[:, 1, :].rearrange("p (m t) -> p t m", t=PAIR).unsqueeze(3).to_broadcast(by_token),
                scalar1=sign[:, 0:1],
                scalar2=None,
                op0=mybir.AluOpType.mult,
            )

        flip_tables()

        bias_flipped = banks.tile([P, P], BF16, tag="bank")
        nc.tensor.transpose(bias_flipped[:], bias_rows[:], ident_bf[:])
        bias_col = keep.tile([P, H], F32)
        nc.scalar.copy(out=bias_col[:], in_=bias_flipped[:, 0:H])

        keep_busy(2)

        def project(first, count):
            acc = banks.tile([P, count, P], F32, tag="bank")
            for j in range(count):
                h = first + j
                for g in range(PASSES):
                    nc.tensor.matmul_mx(
                        out=acc[:, j, :],
                        lhsT=w_words[h // W_LOAD_HEADS][
                            :, g, 2 * (h % W_LOAD_HEADS) * HD : 2 * (h % W_LOAD_HEADS + 1) * HD
                        ].bitcast(FP4X4),
                        lhsT_scale=w_planes[:, g, h * HD : (h + 1) * HD],
                        rhs=x_codes[:, g, :].bitcast(FP8X4),
                        rhs_scale=x_planes[:, g, :],
                        start=(g == 0),
                        stop=(g == PASSES - 1),
                    )
            return acc

        products = []
        whole = [P, 2, PAIR, RUN]

        def head_view(parts, j):
            return parts[:, :, :, j, :]

        def twice(sums):
            return sums.rearrange("p (t r) -> p t r", t=PAIR).unsqueeze(1).to_broadcast(whole)

        both_tables = tables[:].rearrange("p c (t r) -> p c t r", t=PAIR)

        def multiply_on_vector(pair, acc):
            parts = rounds.tile([P, 2, PAIR, PAIR, RUN], F32, tag="parts")
            for j in range(PAIR):
                h = PAIR * pair + j
                nc.vector.scalar_tensor_tensor(
                    out=head_view(parts, j),
                    in0=twice(acc[:, j, :]),
                    scalar=bias_col[:, h : h + 1],
                    in1=both_tables,
                    op0=mybir.AluOpType.add,
                    op1=mybir.AluOpType.mult,
                )
            products.append(parts)

        def multiply_on_gpsimd(pair, acc):
            parts = rounds.tile([P, 2, PAIR, PAIR, RUN], F32, tag="parts")
            for j in range(PAIR):
                h = PAIR * pair + j
                q_sb = rounds.tile([P, P], F32, tag="q_sb")
                nc.scalar.activation(
                    out=q_sb[:],
                    in_=acc[:, j, :],
                    func=mybir.ActivationFunctionType.Identity,
                    bias=bias_col[:, h : h + 1],
                    scale=1.0,
                )
                nc.gpsimd.tensor_tensor(
                    out=head_view(parts, j), in0=twice(q_sb[:]), in1=both_tables, op=mybir.AluOpType.mult
                )
            products.append(parts)

        def join(pair, t, joined):
            parts = products[pair]
            nc.tensor.matmul(
                out=joined,
                lhsT=parts[:, 0, t, :, :].rearrange("p h r -> p (h r)"),
                rhs=ident[:],
                is_transpose=True,
                start=True,
                stop=False,
            )
            nc.tensor.matmul(
                out=joined,
                lhsT=parts[:, 1, t, :, :].rearrange("p h r -> p (h r)"),
                rhs=swap[:].rearrange("p f j -> p (f j)"),
                is_transpose=True,
                start=False,
                stop=True,
            )

        def store(pair, out_sb):
            heads = out[:, PAIR * pair : PAIR * (pair + 1)]
            nc.sync.dma_start(
                out=heads.rearrange("b h (m t) d -> (h m) b (t d)", t=PAIR), in_=out_sb[:].rearrange("p t d -> p (t d)")
            )

        for pair in range(PAIRS):
            acc = project(PAIR * pair, PAIR)
            if pair in GPSIMD_PAIRS:
                multiply_on_gpsimd(pair, acc)
            else:
                multiply_on_vector(pair, acc)
        for pair in JOINS[:-1]:
            out_sb = rounds.tile([P, PAIR, HD], F32, tag="out_sb")
            joined = banks.tile([P, PAIR, HD], F32, tag="bank")
            for t in range(PAIR):
                join(pair, t, joined[:, t, :])
            if pair == JOINS[-2]:
                nc.vector.tensor_copy(out=out_sb[:], in_=joined[:])
            else:
                nc.scalar.copy(out=out_sb[:], in_=joined[:])
            store(pair, out_sb)

        pair = JOINS[-1]
        out_sb = rounds.tile([P, PAIR, HD], F32, tag="out_sb")
        for t in range(PAIR):
            slot = banks.tile([P, HD], F32, tag="bank")
            join(pair, t, slot[:])
            if t == 0:
                nc.scalar.copy(out=out_sb[:, t, :], in_=slot[:])
            else:
                nc.vector.tensor_copy(out=out_sb[:, t, :], in_=slot[:])
        store(pair, out_sb)
